import numpy as np
import ml_dtypes


def mxq(x, axis, fmt="e4m3"):
    dtype, down = {"e4m3": (ml_dtypes.float8_e4m3fn, 7), "e5m2": (ml_dtypes.float8_e5m2, 14)}[fmt]
    v = np.moveaxis(np.asarray(x, np.float32).astype(ml_dtypes.bfloat16).astype(np.float64), axis, -1)
    blocks = v.reshape(v.shape[:-1] + (-1, 32))
    amax = np.abs(blocks).max(-1, keepdims=True)
    byte = np.maximum(np.where(amax > 0, np.frexp(amax)[1] - 1 + 127, 0) - down, 1)
    scale = np.exp2(byte - 127.0)
    codes = (blocks / scale).astype(np.float32).astype(dtype).astype(np.float64)
    return np.moveaxis((codes * scale).reshape(v.shape), -1, axis)


WIDE = False


def mx_kscale(k):
    if not WIDE:
        return np.ones(k)
    levels = np.array([30, -30])
    if k % 512:
        return np.exp2(np.random.permutation(np.resize(levels, k // 32))).repeat(32)
    a = np.empty((k // 512, 16))
    for p in range(k // 512):
        a[p, :8] = np.random.permutation(np.resize(levels, 8))
        for g in range(8):
            far = levels[np.abs(levels - a[p, g]) >= 10]
            a[p, g + 8] = far[np.random.randint(len(far))]
    return np.exp2(a.ravel()).repeat(32)


BF16 = ml_dtypes.bfloat16


def bf(x):
    return np.asarray(x, np.float32).astype(BF16)


def f64(x):
    return np.asarray(x).astype(np.float64)


B, N, DIM, H, KD, D = 4, 256, 1024, 12, 64, 128
HD = 2 * KD + D
HQKV = H * HD
EPS = 1e-5


def setup_inputs():
    s = mx_kscale(DIM)
    c = 2.0 ** (-8.0 * np.random.random(HQKV))
    x = np.random.standard_normal((B, N, DIM)) + 0.5 * np.random.standard_normal(DIM)
    return {"x": bf(x * s),
            "qkv_w": bf(np.random.standard_normal((HQKV, DIM)) * c[:, None] / np.sqrt(DIM) / s),
            "qkv_g": bf(2.0 + 0.2 * np.random.standard_normal(HQKV)),
            "qkv_b": bf(0.3 * np.random.standard_normal(HQKV))}


def bn(y, g, b):
    m = y.mean(axis=(0, 1))
    v = ((y - m) ** 2).mean(axis=(0, 1))
    return (y - m) * (g / np.sqrt(v + EPS)) + b


def reference(x, qkv_w, qkv_g, qkv_b):
    y = mxq(f64(x), 2, "e5m2") @ mxq(f64(qkv_w), 1, "e5m2").T
    qkv = bn(y, f64(qkv_g), f64(qkv_b)).reshape(B, N, H, HD)
    q = qkv[..., :KD].transpose(0, 2, 1, 3)
    k = qkv[..., KD:2 * KD].transpose(0, 2, 1, 3)
    v = qkv[..., 2 * KD:].transpose(0, 2, 1, 3)
    return q, k, v

@@ -1,0 +1,327 @@
+from contextlib import ExitStack
+
+import concourse.mybir as mybir
+from concourse.masks import make_identity
+
+B, N, DIM, H, KD, D = 4, 256, 1024, 12, 64, 128
+HD = 2 * KD + D
+HQKV = H * HD
+EPS = 1e-5
+FLOPS = 2 * B * N * DIM * HQKV
+
+F32 = mybir.dt.float32
+BF16 = mybir.dt.bfloat16
+U32 = mybir.dt.uint32
+U8 = mybir.dt.uint8
+E5X4 = mybir.dt.float8_e5m2_x4
+AF = mybir.ActivationFunctionType
+ALU = mybir.AluOpType
+
+P = 128
+NT = HQKV // P
+NPASS = DIM // 512
+AHEAD = 10
+LAG = 2
+
+
+def tile_attention_pa_kernel(tc, x, qkv_w, qkv_g, qkv_b, out_0, out_1, out_2):
+    nc = tc.nc
+    with ExitStack() as ctx:
+        const = ctx.enter_context(tc.tile_pool(name="const", bufs=1))
+        raw = ctx.enter_context(tc.tile_pool(name="raw", bufs=1))
+        work = ctx.enter_context(tc.tile_pool(name="work", bufs=3))
+        psum = ctx.enter_context(tc.psum_pool(name="psum", bufs=2))
+        ctx.enter_context(tc.manual_schedule())
+
+        one = const.tile([P, 1], F32, name="one", tag="one")
+        nc.vector.memset(one[:], 1.0)
+        warm = const.tile([P, 1], F32, name="warm", tag="warm")
+        nc.scalar.activation(out=warm[:], in_=one[:], func=AF.Abs_reciprocal_sqrt)
+
+        gbraw = const.tile([P, P], BF16, name="gbraw", tag="gbraw")
+        nc.vector.memset(gbraw[:], 0.0)
+
+        identf = const.tile([P, P], F32, name="identf", tag="identf")
+        make_identity(nc, identf[:])
+        identb = const.tile([P, P], BF16, name="identb", tag="identb")
+        make_identity(nc, identb[:])
+
+        xc = const.tile([P, NPASS, B * N], U32, name="xc", tag="xc", align_bytes=64)
+        xs = const.tile([P, NPASS, B * N], U8, name="xs", tag="xs", align_bytes=64)
+        gg = const.tile([P, NT, 2], F32, name="gg", tag="gg")
+        bb = const.tile([P, NT], F32, name="bb", tag="bb")
+
+        xraw = {}
+        wraw = {}
+        bank = {}
+        grp = {}
+        wc = {}
+        ws = {}
+        yb = {}
+        st = {}
+        mv = {}
+        rstd = {}
+        sc2 = {}
+        bia = {}
+        zt = {}
+        ob = {}
+        ot = {}
+
+        def load_x(b):
+            t = raw.tile([P, 2 * DIM], BF16, name="xraw%d" % b, tag="xraw%d" % b)
+            nc.sync.dma_start(out=t[:], in_=x[b, :, :].rearrange("(p e) k -> p (e k)", e=2))
+            xraw[b] = t
+
+        def load_w(i):
+            t = raw.tile([P, DIM], BF16, name="wraw", tag="wraw", bufs=AHEAD + 2)
+            nc.sync.dma_start(out=t[:], in_=qkv_w[i * P : (i + 1) * P, :])
+            wraw[i] = t
+
+        def transposes(key, words, starts, tag, bufs):
+            t = psum.tile([P, 512], F32, name="tp_" + tag, tag=tag, bufs=bufs)
+            for s in range(4):
+                nc.tensor.transpose(
+                    out=t[:, s * P : (s + 1) * P],
+                    in_=words[:, starts[s] : starts[s] + 255 : 2],
+                    identity=identf[:],
+                )
+            bank[key] = t
+
+        def x_transposes(b, g, tag, bufs):
+            words = xraw[b][:].bitcast(F32)
+            transposes(("x", b, g), words, [512 * e + 256 * g + u for e in range(2) for u in range(2)], tag, bufs)
+
+        def w_transposes(i):
+            words = wraw[i][:].bitcast(F32)
+            transposes(("w", i), words, [256 * g + u for g in range(2) for u in range(2)], "w", 2)
+
+        def evacuate(key, copy):
+            t = work.tile([P, 1024], BF16, name="grp", tag="grp", bufs=4, align_bytes=64)
+            copy(
+                out=t[:].bitcast(F32).rearrange("p (a r u) -> p a r u", a=2, u=2),
+                in_=bank[key][:].rearrange("p (a u r) -> p a r u", a=2, u=2),
+            )
+            grp[key] = t
+
+        def x_quantize(b, g):
+            cols = slice(256 * b, 256 * (b + 1))
+            nc.vector.quantize_mx(
+                out=xc[:, g, cols].bitcast(E5X4), scales=xs[:, g, cols], in_=grp[("x", b, g)][:]
+            )
+
+        def w_quantize(i):
+            c = work.tile([P, 256], U32, name="wc", tag="wc", bufs=6, align_bytes=64)
+            s = work.tile([P, 256], U8, name="ws", tag="ws", bufs=6, align_bytes=64)
+            nc.vector.quantize_mx(out=c[:].bitcast(E5X4), scales=s[:], in_=grp[("w", i)][:])
+            wc[i] = c
+            ws[i] = s
+
+        def multiply(i):
+            for hf in range(2):
+                y = psum.tile([P, 512], F32, name="y", tag="y", bufs=4)
+                for g in range(NPASS):
+                    nc.tensor.matmul_mx(
+                        out=y[:],
+                        lhsT=wc[i][:, g * P : (g + 1) * P].bitcast(E5X4),
+                        lhsT_scale=ws[i][:, g * P : (g + 1) * P],
+                        rhs=xc[:, g, hf * 512 : (hf + 1) * 512].bitcast(E5X4),
+                        rhs_scale=xs[:, g, hf * 512 : (hf + 1) * 512],
+                        start=(g == 0),
+                        stop=(g == NPASS - 1),
+                    )
+                yb[(i, hf)] = y
+
+        def stats(i):
+            t = work.tile([P, 2, 6], F32, name="st", tag="st", bufs=3)
+            for hf in range(2):
+                nc.vector.bn_stats(out=t[:, hf, :], in_=yb[(i, hf)][:])
+            st[i] = t
+
+        def aggregate(i):
+            t = work.tile([P, 2], F32, name="mv", tag="mv", bufs=3)
+            nc.vector.bn_aggr(out=t[:], in_=st[i][:].rearrange("p a s -> p (a s)"))
+            mv[i] = t
+
+        def chain_a(i):
+            t = work.tile([P, 1], F32, name="rstd", tag="rstd", bufs=3)
+            nc.scalar.activation(out=t[:], in_=mv[i][:, 1:2], func=AF.Abs_reciprocal_sqrt, bias=EPS, scale=1.0)
+            rstd[i] = t
+
+        def chain_b(i):
+            t = work.tile([P, 2], F32, name="sc2", tag="sc2", bufs=3)
+            nc.scalar.activation(out=t[:], in_=gg[:, i, :], func=AF.Copy, scale=rstd[i][:, 0:1])
+            sc2[i] = t
+
+        def chain_c(i):
+            t = work.tile([P, 1], F32, name="bia", tag="bia", bufs=3)
+            nc.scalar.activation(
+                out=t[:], in_=mv[i][:, 0:1], func=AF.Identity, scale=sc2[i][:, 1:2], bias=bb[:, i : i + 1]
+            )
+            bia[i] = t
+
+        def normalise(i, hf, on_vector):
+            z = work.tile([P, 512], F32, name="z%d" % hf, tag="z%d" % hf, bufs=4)
+            if on_vector:
+                nc.vector.tensor_scalar(
+                    out=z[:], in0=yb[(i, hf)][:], scalar1=sc2[i][:, 0:1], scalar2=bia[i][:, 0:1],
+                    op0=ALU.mult, op1=ALU.add,
+                )
+            else:
+                nc.scalar.activation(
+                    out=z[:], in_=yb[(i, hf)][:], func=AF.Identity, scale=sc2[i][:, 0:1], bias=bia[i][:, 0:1]
+                )
+            zt[(i, hf)] = z
+
+        def back_transposes(i):
+            for hf in range(2):
+                t = psum.tile([P, 512], F32, name="ob", tag="o", bufs=2)
+                for j in range(4):
+                    nc.tensor.transpose(
+                        out=t[:, j * P : (j + 1) * P],
+                        in_=zt[(i, hf)][:, j * P : (j + 1) * P],
+                        identity=identf[:],
+                    )
+                ob[(i, hf)] = t
+
+        def finish(i, hf, on_vector):
+            copy = nc.vector.tensor_copy if on_vector else nc.scalar.copy
+            if hf == 0:
+                ot[i] = work.tile([P, 1024], F32, name="ot", tag="ot", bufs=5)
+            o = ot[i]
+            src = ob[(i, hf)]
+            if i % 2 == 0:
+                copy(
+                    out=o[:].rearrange("p (s j d) -> p s j d", s=2, j=8)[:, :, 4 * hf : 4 * hf + 4, :],
+                    in_=src[:].rearrange("p (j s d) -> p s j d", j=4, s=2),
+                )
+            else:
+                copy(out=o[:, 512 * hf : 512 * (hf + 1)], in_=src[:])
+
+        def store(i, b0, nb):
+            h = i // 2
+            o = ot[i]
+            if i % 2 == 0:
+                for s, dst in enumerate((out_0, out_1)):
+                    nc.sync.dma_start(
+                        out=dst[b0 : b0 + nb, h, :, :].rearrange("b (p e) d -> p b (e d)", e=2),
+                        in_=o[:, 512 * s + 128 * b0 : 512 * s + 128 * (b0 + nb)].rearrange("p (b f) -> p b f", b=nb),
+                    )
+            else:
+                nc.sync.dma_start(
+                    out=out_2[b0 : b0 + nb, h, :, :].rearrange("b (p e) d -> p b (e d)", e=2),
+                    in_=o[:, 256 * b0 : 256 * (b0 + nb)].rearrange("p (b f) -> p b f", b=nb),
+                )
+
+        load_x(0)
+        nc.sync.dma_start(out=gbraw[0:NT, :], in_=qkv_g.rearrange("(c p) -> c p", p=P))
+        nc.sync.dma_start(out=gbraw[32 : 32 + NT, :], in_=qkv_b.rearrange("(c p) -> c p", p=P))
+        load_x(1)
+        load_w(0)
+        load_x(2)
+        load_x(3)
+        for i in range(1, AHEAD):
+            load_w(i)
+
+        vcopy = nc.vector.tensor_copy
+        scopy = nc.scalar.copy
+        x_transposes(0, 0, "y", 4)
+        x_transposes(0, 1, "o", 2)
+        evacuate(("x", 0, 0), vcopy)
+        evacuate(("x", 0, 1), scopy)
+        x_transposes(1, 0, "y", 4)
+        x_transposes(1, 1, "o", 2)
+        evacuate(("x", 1, 0), vcopy)
+        evacuate(("x", 1, 1), scopy)
+        x_quantize(0, 0)
+        x_quantize(0, 1)
+        w_transposes(0)
+        evacuate(("w", 0), scopy)
+        x_quantize(1, 0)
+        x_quantize(1, 1)
+        x_transposes(2, 0, "y", 4)
+        x_transposes(2, 1, "o", 2)
+        evacuate(("x", 2, 0), vcopy)
+        evacuate(("x", 2, 1), scopy)
+        w_quantize(0)
+        x_transposes(3, 0, "y", 4)
+        x_transposes(3, 1, "o", 2)
+        evacuate(("x", 3, 0), vcopy)
+        evacuate(("x", 3, 1), scopy)
+        x_quantize(2, 0)
+        x_quantize(2, 1)
+        w_transposes(1)
+        evacuate(("w", 1), scopy)
+        x_quantize(3, 0)
+        x_quantize(3, 1)
+
+        gps = psum.tile([P, P], BF16, name="gps", tag="w", bufs=2)
+        nc.tensor.transpose(out=gps[:], in_=gbraw[:], identity=identb[:])
+        nc.vector.tensor_copy(out=gg[:, :, 0], in_=gps[:, 0:NT])
+        nc.vector.tensor_scalar(out=gg[:, :, 1], in0=gps[:, 0:NT], scalar1=-1.0, scalar2=None, op0=ALU.mult)
+        nc.vector.tensor_copy(out=bb[:], in_=gps[:, 32 : 32 + NT])
+
+        def fin_on_vector(j):
+            return j % 2 == 1 or j >= 16
+
+        def norm_on_vector(i):
+            return i >= NT - 2
+
+        next_t = 2
+        next_load = AHEAD
+        to_quantize = [1]
+        for i in range(NT + LAG):
+            j = i - LAG
+            back = 0 <= j < NT
+            now_t = []
+            for k in range(2 if i < LAG else 1):
+                if next_t < NT:
+                    now_t.append(next_t)
+                    next_t += 1
+                    if next_load < NT:
+                        load_w(next_load)
+                        next_load += 1
+            if i < NT:
+                multiply(i)
+                stats(i)
+            if 0 <= i - 1 < NT and norm_on_vector(i - 1):
+                normalise(i - 1, 1, True)
+            for k in now_t:
+                w_transposes(k)
+            if to_quantize:
+                w_quantize(to_quantize[0])
+            if i < NT:
+                aggregate(i)
+            for k in to_quantize[1:]:
+                w_quantize(k)
+            to_quantize = []
+            for k in now_t:
+                evacuate(("w", k), scopy if (k < 6 and k % 2 == 1) else vcopy)
+                to_quantize.append(k)
+            if back:
+                back_transposes(j)
+            tail = i >= NT - 2
+            halves = j >= NT - 2
+            if tail and back:
+                finish(j, 0, False)
+                if halves:
+                    store(j, 0, 2)
+                finish(j, 1, fin_on_vector(j))
+            if i < NT:
+                chain_a(i)
+            if back and not tail:
+                finish(j, 0, False)
+            if i < NT:
+                chain_b(i)
+            if back and not tail:
+                finish(j, 1, fin_on_vector(j))
+            if i < NT:
+                chain_c(i)
+            if back:
+                if halves:
+                    store(j, 2, 2)
+                else:
+                    store(j, 0, B)
+            if i < NT:
+                normalise(i, 0, False)
+                if not norm_on_vector(i):
+                    normalise(i, 1, False)

@@ -22,6 +22,7 @@ NT = HQKV // P
 NPASS = DIM // 512
 AHEAD = 10
 LAG = 2
+FIRST_PERM = 4
 
 
 def tile_attention_pa_kernel(tc, x, qkv_w, qkv_g, qkv_b, out_0, out_1, out_2):
@@ -53,6 +54,7 @@ def tile_attention_pa_kernel(tc, x, qkv_w, qkv_g, qkv_b, out_0, out_1, out_2):
 
         xraw = {}
         wraw = {}
+        wperm = {}
         bank = {}
         grp = {}
         wc = {}
@@ -91,9 +93,31 @@ def tile_attention_pa_kernel(tc, x, qkv_w, qkv_g, qkv_b, out_0, out_1, out_2):
             words = xraw[b][:].bitcast(F32)
             transposes(("x", b, g), words, [512 * e + 256 * g + u for e in range(2) for u in range(2)], tag, bufs)
 
+        def w_permute(i):
+            t = work.tile([P, DIM], BF16, name="wperm", tag="wperm", bufs=4)
+            for g in range(NPASS):
+                nc.gpsimd.tensor_scalar(
+                    out=t[:, 512 * g : 512 * (g + 1)].rearrange("p (u m e) -> p u m e", u=2, e=2),
+                    in0=wraw[i][:, 512 * g : 512 * (g + 1)].rearrange("p (m u e) -> p u m e", u=2, e=2),
+                    scalar1=1.0,
+                    scalar2=1.0,
+                    op0=ALU.mult,
+                    op1=ALU.mult,
+                )
+            wperm[i] = t
+
         def w_transposes(i):
-            words = wraw[i][:].bitcast(F32)
-            transposes(("w", i), words, [256 * g + u for g in range(2) for u in range(2)], "w", 2)
+            if i < FIRST_PERM:
+                words = wraw[i][:].bitcast(F32)
+                transposes(("w", i), words, [256 * g + u for g in range(2) for u in range(2)], "w", 2)
+            else:
+                words = wperm[i][:].bitcast(F32)
+                t = psum.tile([P, 512], F32, name="tp_w", tag="w", bufs=2)
+                for s in range(4):
+                    nc.tensor.transpose(
+                        out=t[:, s * P : (s + 1) * P], in_=words[:, s * P : (s + 1) * P], identity=identf[:]
+                    )
+                bank[("w", i)] = t
 
         def evacuate(key, copy):
             t = work.tile([P, 1024], BF16, name="grp", tag="grp", bufs=4, align_bytes=64)
@@ -267,6 +291,7 @@ def tile_attention_pa_kernel(tc, x, qkv_w, qkv_g, qkv_b, out_0, out_1, out_2):
             return i >= NT - 2
 
         next_t = 2
+        next_p = FIRST_PERM
         next_load = AHEAD
         to_quantize = [1]
         for i in range(NT + LAG):
@@ -280,6 +305,10 @@ def tile_attention_pa_kernel(tc, x, qkv_w, qkv_g, qkv_b, out_0, out_1, out_2):
                     if next_load < NT:
                         load_w(next_load)
                         next_load += 1
+            for k in range(3):
+                if next_p < NT and next_p < next_t + 2:
+                    w_permute(next_p)
+                    next_p += 1
             if i < NT:
                 multiply(i)
                 stats(i)

@@ -22,7 +22,6 @@ NT = HQKV // P
 NPASS = DIM // 512
 AHEAD = 10
 LAG = 2
-FIRST_PERM = 4
 
 
 def tile_attention_pa_kernel(tc, x, qkv_w, qkv_g, qkv_b, out_0, out_1, out_2):
@@ -42,6 +41,14 @@ def tile_attention_pa_kernel(tc, x, qkv_w, qkv_g, qkv_b, out_0, out_1, out_2):
         gbraw = const.tile([P, P], BF16, name="gbraw", tag="gbraw")
         nc.vector.memset(gbraw[:], 0.0)
 
+        dz = const.tile([P, 512], BF16, name="dz", tag="dz")
+        nc.vector.memset(dz[:], 0.0)
+
+        def keep_warm(n):
+            t = psum.tile([P, 512], F32, name="warm_ps", tag="w", bufs=2)
+            for r in range(n):
+                nc.tensor.matmul(out=t[:], lhsT=dz[:, 0:P], rhs=dz[:], start=True, stop=True)
+
         identf = const.tile([P, P], F32, name="identf", tag="identf")
         make_identity(nc, identf[:])
         identb = const.tile([P, P], BF16, name="identb", tag="identb")
@@ -54,7 +61,6 @@ def tile_attention_pa_kernel(tc, x, qkv_w, qkv_g, qkv_b, out_0, out_1, out_2):
 
         xraw = {}
         wraw = {}
-        wperm = {}
         bank = {}
         grp = {}
         wc = {}
@@ -93,31 +99,9 @@ def tile_attention_pa_kernel(tc, x, qkv_w, qkv_g, qkv_b, out_0, out_1, out_2):
             words = xraw[b][:].bitcast(F32)
             transposes(("x", b, g), words, [512 * e + 256 * g + u for e in range(2) for u in range(2)], tag, bufs)
 
-        def w_permute(i):
-            t = work.tile([P, DIM], BF16, name="wperm", tag="wperm", bufs=4)
-            for g in range(NPASS):
-                nc.gpsimd.tensor_scalar(
-                    out=t[:, 512 * g : 512 * (g + 1)].rearrange("p (u m e) -> p u m e", u=2, e=2),
-                    in0=wraw[i][:, 512 * g : 512 * (g + 1)].rearrange("p (m u e) -> p u m e", u=2, e=2),
-                    scalar1=1.0,
-                    scalar2=1.0,
-                    op0=ALU.mult,
-                    op1=ALU.mult,
-                )
-            wperm[i] = t
-
         def w_transposes(i):
-            if i < FIRST_PERM:
-                words = wraw[i][:].bitcast(F32)
-                transposes(("w", i), words, [256 * g + u for g in range(2) for u in range(2)], "w", 2)
-            else:
-                words = wperm[i][:].bitcast(F32)
-                t = psum.tile([P, 512], F32, name="tp_w", tag="w", bufs=2)
-                for s in range(4):
-                    nc.tensor.transpose(
-                        out=t[:, s * P : (s + 1) * P], in_=words[:, s * P : (s + 1) * P], identity=identf[:]
-                    )
-                bank[("w", i)] = t
+            words = wraw[i][:].bitcast(F32)
+            transposes(("w", i), words, [256 * g + u for g in range(2) for u in range(2)], "w", 2)
 
         def evacuate(key, copy):
             t = work.tile([P, 1024], BF16, name="grp", tag="grp", bufs=4, align_bytes=64)
@@ -248,12 +232,15 @@ def tile_attention_pa_kernel(tc, x, qkv_w, qkv_g, qkv_b, out_0, out_1, out_2):
 
         vcopy = nc.vector.tensor_copy
         scopy = nc.scalar.copy
+        keep_warm(6)
         x_transposes(0, 0, "y", 4)
         x_transposes(0, 1, "o", 2)
+        keep_warm(2)
         evacuate(("x", 0, 0), vcopy)
         evacuate(("x", 0, 1), scopy)
         x_transposes(1, 0, "y", 4)
         x_transposes(1, 1, "o", 2)
+        keep_warm(2)
         evacuate(("x", 1, 0), vcopy)
         evacuate(("x", 1, 1), scopy)
         x_quantize(0, 0)
@@ -264,11 +251,13 @@ def tile_attention_pa_kernel(tc, x, qkv_w, qkv_g, qkv_b, out_0, out_1, out_2):
         x_quantize(1, 1)
         x_transposes(2, 0, "y", 4)
         x_transposes(2, 1, "o", 2)
+        keep_warm(2)
         evacuate(("x", 2, 0), vcopy)
         evacuate(("x", 2, 1), scopy)
         w_quantize(0)
         x_transposes(3, 0, "y", 4)
         x_transposes(3, 1, "o", 2)
+        keep_warm(2)
         evacuate(("x", 3, 0), vcopy)
         evacuate(("x", 3, 1), scopy)
         x_quantize(2, 0)
@@ -291,7 +280,6 @@ def tile_attention_pa_kernel(tc, x, qkv_w, qkv_g, qkv_b, out_0, out_1, out_2):
             return i >= NT - 2
 
         next_t = 2
-        next_p = FIRST_PERM
         next_load = AHEAD
         to_quantize = [1]
         for i in range(NT + LAG):
@@ -305,10 +293,6 @@ def tile_attention_pa_kernel(tc, x, qkv_w, qkv_g, qkv_b, out_0, out_1, out_2):
                     if next_load < NT:
                         load_w(next_load)
                         next_load += 1
-            for k in range(3):
-                if next_p < NT and next_p < next_t + 2:
-                    w_permute(next_p)
-                    next_p += 1
             if i < NT:
                 multiply(i)
                 stats(i)
@@ -328,6 +312,8 @@ def tile_attention_pa_kernel(tc, x, qkv_w, qkv_g, qkv_b, out_0, out_1, out_2):
                 to_quantize.append(k)
             if back:
                 back_transposes(j)
+                if NT - 3 <= j < NT - 1:
+                    keep_warm(2)
             tail = i >= NT - 2
             halves = j >= NT - 2
             if tail and back:

@@ -41,14 +41,6 @@ def tile_attention_pa_kernel(tc, x, qkv_w, qkv_g, qkv_b, out_0, out_1, out_2):
         gbraw = const.tile([P, P], BF16, name="gbraw", tag="gbraw")
         nc.vector.memset(gbraw[:], 0.0)
 
-        dz = const.tile([P, 512], BF16, name="dz", tag="dz")
-        nc.vector.memset(dz[:], 0.0)
-
-        def keep_warm(n):
-            t = psum.tile([P, 512], F32, name="warm_ps", tag="w", bufs=2)
-            for r in range(n):
-                nc.tensor.matmul(out=t[:], lhsT=dz[:, 0:P], rhs=dz[:], start=True, stop=True)
-
         identf = const.tile([P, P], F32, name="identf", tag="identf")
         make_identity(nc, identf[:])
         identb = const.tile([P, P], BF16, name="identb", tag="identb")
@@ -69,6 +61,7 @@ def tile_attention_pa_kernel(tc, x, qkv_w, qkv_g, qkv_b, out_0, out_1, out_2):
         st = {}
         mv = {}
         rstd = {}
+        nmg = {}
         sc2 = {}
         bia = {}
         zt = {}
@@ -76,32 +69,39 @@ def tile_attention_pa_kernel(tc, x, qkv_w, qkv_g, qkv_b, out_0, out_1, out_2):
         ot = {}
 
         def load_x(b):
-            t = raw.tile([P, 2 * DIM], BF16, name="xraw%d" % b, tag="xraw%d" % b)
-            nc.sync.dma_start(out=t[:], in_=x[b, :, :].rearrange("(p e) k -> p (e k)", e=2))
-            xraw[b] = t
+            for e in range(2):
+                t = raw.tile([P, DIM], BF16, name="xraw%d%d" % (b, e), tag="xraw%d%d" % (b, e))
+                nc.sync.dma_start(out=t[:], in_=x[b, :, :].rearrange("(p e) k -> p e k", e=2)[:, e, :])
+                xraw[(b, e)] = t
 
         def load_w(i):
             t = raw.tile([P, DIM], BF16, name="wraw", tag="wraw", bufs=AHEAD + 2)
             nc.sync.dma_start(out=t[:], in_=qkv_w[i * P : (i + 1) * P, :])
             wraw[i] = t
 
-        def transposes(key, words, starts, tag, bufs):
-            t = psum.tile([P, 512], F32, name="tp_" + tag, tag=tag, bufs=bufs)
-            for s in range(4):
-                nc.tensor.transpose(
-                    out=t[:, s * P : (s + 1) * P],
-                    in_=words[:, starts[s] : starts[s] + 255 : 2],
-                    identity=identf[:],
-                )
-            bank[key] = t
+        def transpose_words(dst, words, first):
+            nc.tensor.transpose(out=dst, in_=words[:, first : first + 255 : 2], identity=identf[:])
 
-        def x_transposes(b, g, tag, bufs):
-            words = xraw[b][:].bitcast(F32)
-            transposes(("x", b, g), words, [512 * e + 256 * g + u for e in range(2) for u in range(2)], tag, bufs)
+        def x_transposes(b):
+            t0 = psum.tile([P, 512], F32, name="tp_x0", tag="y", bufs=5)
+            t1 = psum.tile([P, 512], F32, name="tp_x1", tag="o", bufs=2)
+            for e in range(2):
+                words = xraw[(b, e)][:].bitcast(F32)
+                for g, t in enumerate((t0, t1)):
+                    for u in range(2):
+                        s = 2 * e + u
+                        transpose_words(t[:, s * P : (s + 1) * P], words, 256 * g + u)
+            bank[("x", b, 0)] = t0
+            bank[("x", b, 1)] = t1
 
-        def w_transposes(i):
+        def w_transposes(i, tag, bufs):
             words = wraw[i][:].bitcast(F32)
-            transposes(("w", i), words, [256 * g + u for g in range(2) for u in range(2)], "w", 2)
+            t = psum.tile([P, 512], F32, name="tp_" + tag, tag=tag, bufs=bufs)
+            for g in range(2):
+                for u in range(2):
+                    s = 2 * g + u
+                    transpose_words(t[:, s * P : (s + 1) * P], words, 256 * g + u)
+            bank[("w", i)] = t
 
         def evacuate(key, copy):
             t = work.tile([P, 1024], BF16, name="grp", tag="grp", bufs=4, align_bytes=64)
@@ -126,7 +126,7 @@ def tile_attention_pa_kernel(tc, x, qkv_w, qkv_g, qkv_b, out_0, out_1, out_2):
 
         def multiply(i):
             for hf in range(2):
-                y = psum.tile([P, 512], F32, name="y", tag="y", bufs=4)
+                y = psum.tile([P, 512], F32, name="y", tag="y", bufs=5)
                 for g in range(NPASS):
                     nc.tensor.matmul_mx(
                         out=y[:],
@@ -150,20 +150,21 @@ def tile_attention_pa_kernel(tc, x, qkv_w, qkv_g, qkv_b, out_0, out_1, out_2):
             nc.vector.bn_aggr(out=t[:], in_=st[i][:].rearrange("p a s -> p (a s)"))
             mv[i] = t
 
-        def chain_a(i):
+        def chain_first(i):
+            t = work.tile([P, 1], F32, name="nmg", tag="nmg", bufs=3)
+            nc.scalar.activation(out=t[:], in_=mv[i][:, 0:1], func=AF.Copy, scale=gg[:, i, 1:2])
+            nmg[i] = t
             t = work.tile([P, 1], F32, name="rstd", tag="rstd", bufs=3)
             nc.scalar.activation(out=t[:], in_=mv[i][:, 1:2], func=AF.Abs_reciprocal_sqrt, bias=EPS, scale=1.0)
             rstd[i] = t
 
-        def chain_b(i):
-            t = work.tile([P, 2], F32, name="sc2", tag="sc2", bufs=3)
-            nc.scalar.activation(out=t[:], in_=gg[:, i, :], func=AF.Copy, scale=rstd[i][:, 0:1])
+        def chain_second(i):
+            t = work.tile([P, 1], F32, name="sc", tag="sc", bufs=3)
+            nc.scalar.activation(out=t[:], in_=gg[:, i, 0:1], func=AF.Copy, scale=rstd[i][:, 0:1])
             sc2[i] = t
-
-        def chain_c(i):
             t = work.tile([P, 1], F32, name="bia", tag="bia", bufs=3)
             nc.scalar.activation(
-                out=t[:], in_=mv[i][:, 0:1], func=AF.Identity, scale=sc2[i][:, 1:2], bias=bb[:, i : i + 1]
+                out=t[:], in_=nmg[i][:], func=AF.Identity, scale=rstd[i][:, 0:1], bias=bb[:, i : i + 1]
             )
             bia[i] = t
 
@@ -191,19 +192,19 @@ def tile_attention_pa_kernel(tc, x, qkv_w, qkv_g, qkv_b, out_0, out_1, out_2):
                     )
                 ob[(i, hf)] = t
 
-        def finish(i, hf, on_vector):
+        def finish(i, hf, on_vector, j0=0, nj=4):
             copy = nc.vector.tensor_copy if on_vector else nc.scalar.copy
-            if hf == 0:
+            if i not in ot:
                 ot[i] = work.tile([P, 1024], F32, name="ot", tag="ot", bufs=5)
             o = ot[i]
-            src = ob[(i, hf)]
+            src = ob[(i, hf)][:, P * j0 : P * (j0 + nj)]
             if i % 2 == 0:
                 copy(
-                    out=o[:].rearrange("p (s j d) -> p s j d", s=2, j=8)[:, :, 4 * hf : 4 * hf + 4, :],
-                    in_=src[:].rearrange("p (j s d) -> p s j d", j=4, s=2),
+                    out=o[:].rearrange("p (s j d) -> p s j d", s=2, j=8)[:, :, 4 * hf + j0 : 4 * hf + j0 + nj, :],
+                    in_=src.rearrange("p (j s d) -> p s j d", j=nj, s=2),
                 )
             else:
-                copy(out=o[:, 512 * hf : 512 * (hf + 1)], in_=src[:])
+                copy(out=o[:, 512 * hf + P * j0 : 512 * hf + P * (j0 + nj)], in_=src)
 
         def store(i, b0, nb):
             h = i // 2
@@ -232,46 +233,36 @@ def tile_attention_pa_kernel(tc, x, qkv_w, qkv_g, qkv_b, out_0, out_1, out_2):
 
         vcopy = nc.vector.tensor_copy
         scopy = nc.scalar.copy
-        keep_warm(6)
-        x_transposes(0, 0, "y", 4)
-        x_transposes(0, 1, "o", 2)
-        keep_warm(2)
+        x_transposes(0)
         evacuate(("x", 0, 0), vcopy)
         evacuate(("x", 0, 1), scopy)
-        x_transposes(1, 0, "y", 4)
-        x_transposes(1, 1, "o", 2)
-        keep_warm(2)
+        x_transposes(1)
         evacuate(("x", 1, 0), vcopy)
         evacuate(("x", 1, 1), scopy)
         x_quantize(0, 0)
         x_quantize(0, 1)
-        w_transposes(0)
+        w_transposes(0, "w", 1)
         evacuate(("w", 0), scopy)
+        gps = psum.tile([P, P], BF16, name="gps", tag="y", bufs=5)
+        nc.tensor.transpose(out=gps[:], in_=gbraw[:], identity=identb[:])
         x_quantize(1, 0)
         x_quantize(1, 1)
-        x_transposes(2, 0, "y", 4)
-        x_transposes(2, 1, "o", 2)
-        keep_warm(2)
+        nc.vector.tensor_copy(out=gg[:, :, 0], in_=gps[:, 0:NT])
+        nc.vector.tensor_scalar(out=gg[:, :, 1], in0=gps[:, 0:NT], scalar1=-1.0, scalar2=None, op0=ALU.mult)
+        nc.vector.tensor_copy(out=bb[:], in_=gps[:, 32 : 32 + NT])
+        x_transposes(2)
         evacuate(("x", 2, 0), vcopy)
         evacuate(("x", 2, 1), scopy)
         w_quantize(0)
-        x_transposes(3, 0, "y", 4)
-        x_transposes(3, 1, "o", 2)
-        keep_warm(2)
+        x_transposes(3)
         evacuate(("x", 3, 0), vcopy)
         evacuate(("x", 3, 1), scopy)
         x_quantize(2, 0)
         x_quantize(2, 1)
-        w_transposes(1)
+        w_transposes(1, "w", 1)
         evacuate(("w", 1), scopy)
         x_quantize(3, 0)
         x_quantize(3, 1)
-
-        gps = psum.tile([P, P], BF16, name="gps", tag="w", bufs=2)
-        nc.tensor.transpose(out=gps[:], in_=gbraw[:], identity=identb[:])
-        nc.vector.tensor_copy(out=gg[:, :, 0], in_=gps[:, 0:NT])
-        nc.vector.tensor_scalar(out=gg[:, :, 1], in0=gps[:, 0:NT], scalar1=-1.0, scalar2=None, op0=ALU.mult)
-        nc.vector.tensor_copy(out=bb[:], in_=gps[:, 32 : 32 + NT])
 
         def fin_on_vector(j):
             return j % 2 == 1 or j >= 16
@@ -298,8 +289,11 @@ def tile_attention_pa_kernel(tc, x, qkv_w, qkv_g, qkv_b, out_0, out_1, out_2):
                 stats(i)
             if 0 <= i - 1 < NT and norm_on_vector(i - 1):
                 normalise(i - 1, 1, True)
-            for k in now_t:
-                w_transposes(k)
+            for n, k in enumerate(now_t):
+                if n == 0:
+                    w_transposes(k, "w", 1)
+                else:
+                    w_transposes(k, "o", 2)
             if to_quantize:
                 w_quantize(to_quantize[0])
             if i < NT:
@@ -312,25 +306,27 @@ def tile_attention_pa_kernel(tc, x, qkv_w, qkv_g, qkv_b, out_0, out_1, out_2):
                 to_quantize.append(k)
             if back:
                 back_transposes(j)
-                if NT - 3 <= j < NT - 1:
-                    keep_warm(2)
             tail = i >= NT - 2
             halves = j >= NT - 2
+            on_v = back and fin_on_vector(j)
             if tail and back:
                 finish(j, 0, False)
                 if halves:
                     store(j, 0, 2)
-                finish(j, 1, fin_on_vector(j))
+                finish(j, 1, on_v)
             if i < NT:
-                chain_a(i)
+                chain_first(i)
             if back and not tail:
-                finish(j, 0, False)
+                if on_v:
+                    finish(j, 0, False, 0, 2)
+                else:
+                    finish(j, 0, False)
             if i < NT:
-                chain_b(i)
+                chain_second(i)
             if back and not tail:
-                finish(j, 1, fin_on_vector(j))
-            if i < NT:
-                chain_c(i)
+                if on_v:
+                    finish(j, 0, False, 2, 2)
+                finish(j, 1, on_v)
             if back:
                 if halves:
                     store(j, 2, 2)

@@ -22,6 +22,7 @@ NT = HQKV // P
 NPASS = DIM // 512
 AHEAD = 10
 LAG = 2
+FIRST_SORTED = 6
 
 
 def tile_attention_pa_kernel(tc, x, qkv_w, qkv_g, qkv_b, out_0, out_1, out_2):
@@ -53,6 +54,7 @@ def tile_attention_pa_kernel(tc, x, qkv_w, qkv_g, qkv_b, out_0, out_1, out_2):
 
         xraw = {}
         wraw = {}
+        wsort = {}
         bank = {}
         grp = {}
         wc = {}
@@ -82,6 +84,19 @@ def tile_attention_pa_kernel(tc, x, qkv_w, qkv_g, qkv_b, out_0, out_1, out_2):
         def transpose_words(dst, words, first):
             nc.tensor.transpose(out=dst, in_=words[:, first : first + 255 : 2], identity=identf[:])
 
+        def sort_words(i, tick):
+            t = raw.tile([P, DIM], BF16, name="wsort", tag="wsort", bufs=4)
+            for g in range(NPASS):
+                nc.gpsimd.tensor_scalar(
+                    out=t[:, 512 * g : 512 * (g + 1)].rearrange("p (u m e) -> p u m e", u=2, e=2),
+                    in0=wraw[i][:, 512 * g : 512 * (g + 1)].rearrange("p (m u e) -> p u m e", u=2, e=2),
+                    scalar1=tick[:, 0:1],
+                    scalar2=1.0,
+                    op0=ALU.mult,
+                    op1=ALU.mult,
+                )
+            wsort[i] = t
+
         def x_transposes(b):
             t0 = psum.tile([P, 512], F32, name="tp_x0", tag="y", bufs=5)
             t1 = psum.tile([P, 512], F32, name="tp_x1", tag="o", bufs=2)
@@ -95,12 +110,19 @@ def tile_attention_pa_kernel(tc, x, qkv_w, qkv_g, qkv_b, out_0, out_1, out_2):
             bank[("x", b, 1)] = t1
 
         def w_transposes(i, tag, bufs):
-            words = wraw[i][:].bitcast(F32)
             t = psum.tile([P, 512], F32, name="tp_" + tag, tag=tag, bufs=bufs)
-            for g in range(2):
-                for u in range(2):
-                    s = 2 * g + u
-                    transpose_words(t[:, s * P : (s + 1) * P], words, 256 * g + u)
+            if i in wsort:
+                words = wsort[i][:].bitcast(F32)
+                for s in range(4):
+                    nc.tensor.transpose(
+                        out=t[:, s * P : (s + 1) * P], in_=words[:, s * P : (s + 1) * P], identity=identf[:]
+                    )
+            else:
+                words = wraw[i][:].bitcast(F32)
+                for g in range(2):
+                    for u in range(2):
+                        s = 2 * g + u
+                        transpose_words(t[:, s * P : (s + 1) * P], words, 256 * g + u)
             bank[("w", i)] = t
 
         def evacuate(key, copy):
@@ -296,6 +318,10 @@ def tile_attention_pa_kernel(tc, x, qkv_w, qkv_g, qkv_b, out_0, out_1, out_2):
                     w_transposes(k, "o", 2)
             if to_quantize:
                 w_quantize(to_quantize[0])
+            if i + FIRST_SORTED < NT:
+                tick = work.tile([P, 1], F32, name="tick", tag="tick", bufs=3)
+                nc.vector.memset(tick[:], 1.0)
+                sort_words(i + FIRST_SORTED, tick)
             if i < NT:
                 aggregate(i)
             for k in to_quantize[1:]:

@@ -84,14 +84,14 @@ def tile_attention_pa_kernel(tc, x, qkv_w, qkv_g, qkv_b, out_0, out_1, out_2):
         def transpose_words(dst, words, first):
             nc.tensor.transpose(out=dst, in_=words[:, first : first + 255 : 2], identity=identf[:])
 
-        def sort_words(i, tick):
+        def sort_words(i, count):
             t = raw.tile([P, DIM], BF16, name="wsort", tag="wsort", bufs=4)
             for g in range(NPASS):
                 nc.gpsimd.tensor_scalar(
                     out=t[:, 512 * g : 512 * (g + 1)].rearrange("p (u m e) -> p u m e", u=2, e=2),
                     in0=wraw[i][:, 512 * g : 512 * (g + 1)].rearrange("p (m u e) -> p u m e", u=2, e=2),
-                    scalar1=tick[:, 0:1],
-                    scalar2=1.0,
+                    scalar1=1.0 / 256.0,
+                    scalar2=count,
                     op0=ALU.mult,
                     op1=ALU.mult,
                 )
@@ -319,9 +319,7 @@ def tile_attention_pa_kernel(tc, x, qkv_w, qkv_g, qkv_b, out_0, out_1, out_2):
             if to_quantize:
                 w_quantize(to_quantize[0])
             if i + FIRST_SORTED < NT:
-                tick = work.tile([P, 1], F32, name="tick", tag="tick", bufs=3)
-                nc.vector.memset(tick[:], 1.0)
-                sort_words(i + FIRST_SORTED, tick)
+                sort_words(i + FIRST_SORTED, st[i][:, 1, 0:1])
             if i < NT:
                 aggregate(i)
             for k in to_quantize[1:]:

@@ -205,7 +205,8 @@ def tile_attention_pa_kernel(tc, x, qkv_w, qkv_g, qkv_b, out_0, out_1, out_2):
 
         def back_transposes(i):
             for hf in range(2):
-                t = psum.tile([P, 512], F32, name="ob", tag="o", bufs=2)
+                third = i >= NT - 6 and (2 * i + hf) % 3 == 2
+                t = psum.tile([P, 512], F32, name="ob", tag="w" if third else "o", bufs=1 if third else 2)
                 for j in range(4):
                     nc.tensor.transpose(
                         out=t[:, j * P : (j + 1) * P],
@@ -287,7 +288,7 @@ def tile_attention_pa_kernel(tc, x, qkv_w, qkv_g, qkv_b, out_0, out_1, out_2):
         x_quantize(3, 1)
 
         def fin_on_vector(j):
-            return j % 2 == 1 or j >= 16
+            return j % 2 == 1 or j >= 18
 
         def norm_on_vector(i):
             return i >= NT - 2

@@ -245,13 +245,14 @@ def tile_attention_pa_kernel(tc, x, qkv_w, qkv_g, qkv_b, out_0, out_1, out_2):
                 )
 
         load_x(0)
-        nc.sync.dma_start(out=gbraw[0:NT, :], in_=qkv_g.rearrange("(c p) -> c p", p=P))
-        nc.sync.dma_start(out=gbraw[32 : 32 + NT, :], in_=qkv_b.rearrange("(c p) -> c p", p=P))
         load_x(1)
         load_w(0)
         load_x(2)
         load_x(3)
-        for i in range(1, AHEAD):
+        load_w(1)
+        nc.sync.dma_start(out=gbraw[0:NT, :], in_=qkv_g.rearrange("(c p) -> c p", p=P))
+        nc.sync.dma_start(out=gbraw[32 : 32 + NT, :], in_=qkv_b.rearrange("(c p) -> c p", p=P))
+        for i in range(2, AHEAD):
             load_w(i)
 
         vcopy = nc.vector.tensor_copy
@@ -266,13 +267,8 @@ def tile_attention_pa_kernel(tc, x, qkv_w, qkv_g, qkv_b, out_0, out_1, out_2):
         x_quantize(0, 1)
         w_transposes(0, "w", 1)
         evacuate(("w", 0), scopy)
-        gps = psum.tile([P, P], BF16, name="gps", tag="y", bufs=5)
-        nc.tensor.transpose(out=gps[:], in_=gbraw[:], identity=identb[:])
         x_quantize(1, 0)
         x_quantize(1, 1)
-        nc.vector.tensor_copy(out=gg[:, :, 0], in_=gps[:, 0:NT])
-        nc.vector.tensor_scalar(out=gg[:, :, 1], in0=gps[:, 0:NT], scalar1=-1.0, scalar2=None, op0=ALU.mult)
-        nc.vector.tensor_copy(out=bb[:], in_=gps[:, 32 : 32 + NT])
         x_transposes(2)
         evacuate(("x", 2, 0), vcopy)
         evacuate(("x", 2, 1), scopy)
@@ -317,6 +313,12 @@ def tile_attention_pa_kernel(tc, x, qkv_w, qkv_g, qkv_b, out_0, out_1, out_2):
                     w_transposes(k, "w", 1)
                 else:
                     w_transposes(k, "o", 2)
+            if i == 0:
+                gps = psum.tile([P, P], BF16, name="gps", tag="o", bufs=2)
+                nc.tensor.transpose(out=gps[:], in_=gbraw[:], identity=identb[:])
+                nc.scalar.copy(out=gg[:, :, 0], in_=gps[:, 0:NT])
+                nc.scalar.activation(out=gg[:, :, 1], in_=gps[:, 0:NT], func=AF.Copy, scale=-1.0)
+                nc.scalar.copy(out=bb[:], in_=gps[:, 32 : 32 + NT])
             if to_quantize:
                 w_quantize(to_quantize[0])
             if i + FIRST_SORTED < NT:

@@ -76,6 +76,15 @@ def tile_attention_pa_kernel(tc, x, qkv_w, qkv_g, qkv_b, out_0, out_1, out_2):
                 nc.sync.dma_start(out=t[:], in_=x[b, :, :].rearrange("(p e) k -> p e k", e=2)[:, e, :])
                 xraw[(b, e)] = t
 
+        def load_x_by_pass(b):
+            for g in range(NPASS):
+                for e in range(2):
+                    t = raw.tile([P, 512], BF16, name="xraw%d%d%d" % (b, e, g), tag="xraw%d%d%d" % (b, e, g))
+                    nc.sync.dma_start(
+                        out=t[:], in_=x[b, :, :].rearrange("(p e) k -> p e k", e=2)[:, e, 512 * g : 512 * (g + 1)]
+                    )
+                    xraw[(b, e, g)] = t
+
         def load_w(i):
             t = raw.tile([P, DIM], BF16, name="wraw", tag="wraw", bufs=AHEAD + 2)
             nc.sync.dma_start(out=t[:], in_=qkv_w[i * P : (i + 1) * P, :])
@@ -96,6 +105,18 @@ def tile_attention_pa_kernel(tc, x, qkv_w, qkv_g, qkv_b, out_0, out_1, out_2):
                     op1=ALU.mult,
                 )
             wsort[i] = t
+
+        def x_transposes_by_pass(b):
+            t0 = psum.tile([P, 512], F32, name="tp_x0", tag="y", bufs=5)
+            t1 = psum.tile([P, 512], F32, name="tp_x1", tag="o", bufs=2)
+            for g, t in enumerate((t0, t1)):
+                for e in range(2):
+                    words = xraw[(b, e, g)][:].bitcast(F32)
+                    for u in range(2):
+                        s = 2 * e + u
+                        transpose_words(t[:, s * P : (s + 1) * P], words, u)
+            bank[("x", b, 0)] = t0
+            bank[("x", b, 1)] = t1
 
         def x_transposes(b):
             t0 = psum.tile([P, 512], F32, name="tp_x0", tag="y", bufs=5)
@@ -248,10 +269,12 @@ def tile_attention_pa_kernel(tc, x, qkv_w, qkv_g, qkv_b, out_0, out_1, out_2):
         load_x(1)
         load_w(0)
         load_x(2)
-        load_x(3)
+        load_x_by_pass(3)
         load_w(1)
-        nc.sync.dma_start(out=gbraw[0:NT, :], in_=qkv_g.rearrange("(c p) -> c p", p=P))
-        nc.sync.dma_start(out=gbraw[32 : 32 + NT, :], in_=qkv_b.rearrange("(c p) -> c p", p=P))
+        for r0, src in ((0, qkv_g), (32, qkv_b)):
+            rows = src.rearrange("(c p) -> c p", p=P)
+            nc.sync.dma_start(out=gbraw[r0 : r0 + 16, :], in_=rows[0:16, :])
+            nc.sync.dma_start(out=gbraw[r0 + 16 : r0 + NT, :], in_=rows[16:NT, :])
         for i in range(2, AHEAD):
             load_w(i)
 
@@ -269,18 +292,18 @@ def tile_attention_pa_kernel(tc, x, qkv_w, qkv_g, qkv_b, out_0, out_1, out_2):
         evacuate(("w", 0), scopy)
         x_quantize(1, 0)
         x_quantize(1, 1)
-        x_transposes(2)
-        evacuate(("x", 2, 0), vcopy)
-        evacuate(("x", 2, 1), scopy)
         w_quantize(0)
-        x_transposes(3)
+        x_transposes(2)
+        evacuate(("x", 2, 1), scopy)
+        evacuate(("x", 2, 0), scopy)
+        x_transposes_by_pass(3)
         evacuate(("x", 3, 0), vcopy)
         evacuate(("x", 3, 1), scopy)
-        x_quantize(2, 0)
         x_quantize(2, 1)
+        x_quantize(2, 0)
+        x_quantize(3, 0)
         w_transposes(1, "w", 1)
         evacuate(("w", 1), scopy)
-        x_quantize(3, 0)
         x_quantize(3, 1)
 
         def fin_on_vector(j):
@@ -340,7 +363,12 @@ def tile_attention_pa_kernel(tc, x, qkv_w, qkv_g, qkv_b, out_0, out_1, out_2):
                 finish(j, 0, False)
                 if halves:
                     store(j, 0, 2)
-                finish(j, 1, on_v)
+                if j == NT - 1:
+                    finish(j, 1, on_v, 0, 2)
+                    store(j, 2, 1)
+                    finish(j, 1, on_v, 2, 2)
+                else:
+                    finish(j, 1, on_v)
             if i < NT:
                 chain_first(i)
             if back and not tail:
@@ -355,7 +383,9 @@ def tile_attention_pa_kernel(tc, x, qkv_w, qkv_g, qkv_b, out_0, out_1, out_2):
                     finish(j, 0, False, 2, 2)
                 finish(j, 1, on_v)
             if back:
-                if halves:
+                if j == NT - 1:
+                    store(j, 3, 1)
+                elif halves:
                     store(j, 2, 2)
                 else:
                     store(j, 0, B)

@@ -357,7 +357,7 @@ def tile_attention_pa_kernel(tc, x, qkv_w, qkv_g, qkv_b, out_0, out_1, out_2):
             if back:
                 back_transposes(j)
             tail = i >= NT - 2
-            halves = j >= NT - 2
+            halves = j >= NT - 1
             on_v = back and fin_on_vector(j)
             if tail and back:
                 finish(j, 0, False)

@@ -167,8 +167,8 @@ def tile_attention_pa_kernel(tc, x, qkv_w, qkv_g, qkv_b, out_0, out_1, out_2):
             wc[i] = c
             ws[i] = s
 
-        def multiply(i):
-            for hf in range(2):
+        def multiply(i, halves=(0, 1)):
+            for hf in halves:
                 y = psum.tile([P, 512], F32, name="y", tag="y", bufs=5)
                 for g in range(NPASS):
                     nc.tensor.matmul_mx(
@@ -302,6 +302,7 @@ def tile_attention_pa_kernel(tc, x, qkv_w, qkv_g, qkv_b, out_0, out_1, out_2):
         x_quantize(2, 1)
         x_quantize(2, 0)
         x_quantize(3, 0)
+        multiply(0, (0,))
         w_transposes(1, "w", 1)
         evacuate(("w", 1), scopy)
         x_quantize(3, 1)
@@ -327,7 +328,7 @@ def tile_attention_pa_kernel(tc, x, qkv_w, qkv_g, qkv_b, out_0, out_1, out_2):
                         load_w(next_load)
                         next_load += 1
             if i < NT:
-                multiply(i)
+                multiply(i, (1,) if i == 0 else (0, 1))
                 stats(i)
             if 0 <= i - 1 < NT and norm_on_vector(i - 1):
                 normalise(i - 1, 1, True)

@@ -211,6 +211,23 @@ def tile_attention_pa_kernel(tc, x, qkv_w, qkv_g, qkv_b, out_0, out_1, out_2):
             )
             bia[i] = t
 
+        def chain_rstd(i):
+            t = work.tile([P, 1], F32, name="rstd", tag="rstd", bufs=3)
+            nc.scalar.activation(out=t[:], in_=mv[i][:, 1:2], func=AF.Abs_reciprocal_sqrt, bias=EPS, scale=1.0)
+            rstd[i] = t
+
+        def chain_scales(i):
+            t = work.tile([P, 2], F32, name="scn", tag="scn", bufs=3)
+            nc.scalar.activation(out=t[:], in_=gg[:, i, :], func=AF.Copy, scale=rstd[i][:, 0:1])
+            sc2[i] = t
+
+        def chain_bias(i):
+            t = work.tile([P, 1], F32, name="bia", tag="bia", bufs=3)
+            nc.scalar.activation(
+                out=t[:], in_=mv[i][:, 0:1], func=AF.Identity, scale=sc2[i][:, 1:2], bias=bb[:, i : i + 1]
+            )
+            bia[i] = t
+
         def normalise(i, hf, on_vector):
             z = work.tile([P, 512], F32, name="z%d" % hf, tag="z%d" % hf, bufs=4)
             if on_vector:
@@ -370,19 +387,25 @@ def tile_attention_pa_kernel(tc, x, qkv_w, qkv_g, qkv_b, out_0, out_1, out_2):
                     finish(j, 1, on_v, 2, 2)
                 else:
                     finish(j, 1, on_v)
-            if i < NT:
-                chain_first(i)
-            if back and not tail:
-                if on_v:
+            level = back and j < 18
+            if level:
+                chain_rstd(i)
+                finish(j, 0, False, 0, 2)
+                chain_scales(i)
+                finish(j, 0, False, 2, 2)
+                chain_bias(i)
+                finish(j, 1, True, 0, 2)
+                finish(j, 1, False, 2, 2)
+            else:
+                if i < NT:
+                    chain_first(i)
+                if back and not tail:
                     finish(j, 0, False, 0, 2)
-                else:
-                    finish(j, 0, False)
-            if i < NT:
-                chain_second(i)
-            if back and not tail:
-                if on_v:
+                if i < NT:
+                    chain_second(i)
+                if back and not tail:
                     finish(j, 0, False, 2, 2)
-                finish(j, 1, on_v)
+                    finish(j, 1, on_v)
             if back:
                 if j == NT - 1:
                     store(j, 3, 1)

@@ -394,8 +394,10 @@ def tile_attention_pa_kernel(tc, x, qkv_w, qkv_g, qkv_b, out_0, out_1, out_2):
                 chain_scales(i)
                 finish(j, 0, False, 2, 2)
                 chain_bias(i)
-                finish(j, 1, True, 0, 2)
-                finish(j, 1, False, 2, 2)
+                nv = 3 if j % 2 == 1 else 0
+                if nv:
+                    finish(j, 1, True, 0, nv)
+                finish(j, 1, False, nv, 4 - nv)
             else:
                 if i < NT:
                     chain_first(i)

@@ -47,8 +47,8 @@ def tile_attention_pa_kernel(tc, x, qkv_w, qkv_g, qkv_b, out_0, out_1, out_2):
         identb = const.tile([P, P], BF16, name="identb", tag="identb")
         make_identity(nc, identb[:])
 
-        xc = const.tile([P, NPASS, B * N], U32, name="xc", tag="xc", align_bytes=64)
-        xs = const.tile([P, NPASS, B * N], U8, name="xs", tag="xs", align_bytes=64)
+        xc = const.tile([P, NPASS, B * N], U32, name="xc", tag="xc", align_bytes=256)
+        xs = const.tile([P, NPASS, B * N], U8, name="xs", tag="xs", align_bytes=256)
         gg = const.tile([P, NT, 2], F32, name="gg", tag="gg")
         bb = const.tile([P, NT], F32, name="bb", tag="bb")
 
@@ -147,7 +147,7 @@ def tile_attention_pa_kernel(tc, x, qkv_w, qkv_g, qkv_b, out_0, out_1, out_2):
             bank[("w", i)] = t
 
         def evacuate(key, copy):
-            t = work.tile([P, 1024], BF16, name="grp", tag="grp", bufs=4, align_bytes=64)
+            t = work.tile([P, 1024], BF16, name="grp", tag="grp", bufs=4, align_bytes=256)
             copy(
                 out=t[:].bitcast(F32).rearrange("p (a r u) -> p a r u", a=2, u=2),
                 in_=bank[key][:].rearrange("p (a u r) -> p a r u", a=2, u=2),
@@ -161,8 +161,8 @@ def tile_attention_pa_kernel(tc, x, qkv_w, qkv_g, qkv_b, out_0, out_1, out_2):
             )
 
         def w_quantize(i):
-            c = work.tile([P, 256], U32, name="wc", tag="wc", bufs=6, align_bytes=64)
-            s = work.tile([P, 256], U8, name="ws", tag="ws", bufs=6, align_bytes=64)
+            c = work.tile([P, 256], U32, name="wc", tag="wc", bufs=6, align_bytes=256)
+            s = work.tile([P, 256], U8, name="ws", tag="ws", bufs=6, align_bytes=256)
             nc.vector.quantize_mx(out=c[:].bitcast(E5X4), scales=s[:], in_=grp[("w", i)][:])
             wc[i] = c
             ws[i] = s

@@ -23,6 +23,7 @@ NPASS = DIM // 512
 AHEAD = 10
 LAG = 2
 FIRST_SORTED = 6
+FT = list(range(21)) + [22, 21, 23]
 
 
 def tile_attention_pa_kernel(tc, x, qkv_w, qkv_g, qkv_b, out_0, out_1, out_2):
@@ -87,7 +88,7 @@ def tile_attention_pa_kernel(tc, x, qkv_w, qkv_g, qkv_b, out_0, out_1, out_2):
 
         def load_w(i):
             t = raw.tile([P, DIM], BF16, name="wraw", tag="wraw", bufs=AHEAD + 2)
-            nc.sync.dma_start(out=t[:], in_=qkv_w[i * P : (i + 1) * P, :])
+            nc.sync.dma_start(out=t[:], in_=qkv_w[FT[i] * P : (FT[i] + 1) * P, :])
             wraw[i] = t
 
         def transpose_words(dst, words, first):
@@ -195,7 +196,7 @@ def tile_attention_pa_kernel(tc, x, qkv_w, qkv_g, qkv_b, out_0, out_1, out_2):
 
         def chain_first(i):
             t = work.tile([P, 1], F32, name="nmg", tag="nmg", bufs=3)
-            nc.scalar.activation(out=t[:], in_=mv[i][:, 0:1], func=AF.Copy, scale=gg[:, i, 1:2])
+            nc.scalar.activation(out=t[:], in_=mv[i][:, 0:1], func=AF.Copy, scale=gg[:, FT[i], 1:2])
             nmg[i] = t
             t = work.tile([P, 1], F32, name="rstd", tag="rstd", bufs=3)
             nc.scalar.activation(out=t[:], in_=mv[i][:, 1:2], func=AF.Abs_reciprocal_sqrt, bias=EPS, scale=1.0)
@@ -203,11 +204,11 @@ def tile_attention_pa_kernel(tc, x, qkv_w, qkv_g, qkv_b, out_0, out_1, out_2):
 
         def chain_second(i):
             t = work.tile([P, 1], F32, name="sc", tag="sc", bufs=3)
-            nc.scalar.activation(out=t[:], in_=gg[:, i, 0:1], func=AF.Copy, scale=rstd[i][:, 0:1])
+            nc.scalar.activation(out=t[:], in_=gg[:, FT[i], 0:1], func=AF.Copy, scale=rstd[i][:, 0:1])
             sc2[i] = t
             t = work.tile([P, 1], F32, name="bia", tag="bia", bufs=3)
             nc.scalar.activation(
-                out=t[:], in_=nmg[i][:], func=AF.Identity, scale=rstd[i][:, 0:1], bias=bb[:, i : i + 1]
+                out=t[:], in_=nmg[i][:], func=AF.Identity, scale=rstd[i][:, 0:1], bias=bb[:, FT[i] : FT[i] + 1]
             )
             bia[i] = t
 
@@ -218,13 +219,13 @@ def tile_attention_pa_kernel(tc, x, qkv_w, qkv_g, qkv_b, out_0, out_1, out_2):
 
         def chain_scales(i):
             t = work.tile([P, 2], F32, name="scn", tag="scn", bufs=3)
-            nc.scalar.activation(out=t[:], in_=gg[:, i, :], func=AF.Copy, scale=rstd[i][:, 0:1])
+            nc.scalar.activation(out=t[:], in_=gg[:, FT[i], :], func=AF.Copy, scale=rstd[i][:, 0:1])
             sc2[i] = t
 
         def chain_bias(i):
             t = work.tile([P, 1], F32, name="bia", tag="bia", bufs=3)
             nc.scalar.activation(
-                out=t[:], in_=mv[i][:, 0:1], func=AF.Identity, scale=sc2[i][:, 1:2], bias=bb[:, i : i + 1]
+                out=t[:], in_=mv[i][:, 0:1], func=AF.Identity, scale=sc2[i][:, 1:2], bias=bb[:, FT[i] : FT[i] + 1]
             )
             bia[i] = t
 
@@ -259,7 +260,7 @@ def tile_attention_pa_kernel(tc, x, qkv_w, qkv_g, qkv_b, out_0, out_1, out_2):
                 ot[i] = work.tile([P, 1024], F32, name="ot", tag="ot", bufs=5)
             o = ot[i]
             src = ob[(i, hf)][:, P * j0 : P * (j0 + nj)]
-            if i % 2 == 0:
+            if FT[i] % 2 == 0:
                 copy(
                     out=o[:].rearrange("p (s j d) -> p s j d", s=2, j=8)[:, :, 4 * hf + j0 : 4 * hf + j0 + nj, :],
                     in_=src.rearrange("p (j s d) -> p s j d", j=nj, s=2),
@@ -268,9 +269,9 @@ def tile_attention_pa_kernel(tc, x, qkv_w, qkv_g, qkv_b, out_0, out_1, out_2):
                 copy(out=o[:, 512 * hf + P * j0 : 512 * hf + P * (j0 + nj)], in_=src)
 
         def store(i, b0, nb):
-            h = i // 2
+            h = FT[i] // 2
             o = ot[i]
-            if i % 2 == 0:
+            if FT[i] % 2 == 0:
                 for s, dst in enumerate((out_0, out_1)):
                     nc.sync.dma_start(
                         out=dst[b0 : b0 + nb, h, :, :].rearrange("b (p e) d -> p b (e d)", e=2),
@@ -323,6 +324,11 @@ def tile_attention_pa_kernel(tc, x, qkv_w, qkv_g, qkv_b, out_0, out_1, out_2):
         w_transposes(1, "w", 1)
         evacuate(("w", 1), scopy)
         x_quantize(3, 1)
+        gps = psum.tile([P, P], BF16, name="gps", tag="o", bufs=2)
+        nc.tensor.transpose(out=gps[:], in_=gbraw[:], identity=identb[:])
+        nc.scalar.copy(out=gg[:, :, 0], in_=gps[:, 0:NT])
+        nc.scalar.activation(out=gg[:, :, 1], in_=gps[:, 0:NT], func=AF.Copy, scale=-1.0)
+        nc.scalar.copy(out=bb[:], in_=gps[:, 32 : 32 + NT])
 
         def fin_on_vector(j):
             return j % 2 == 1 or j >= 18
@@ -354,12 +360,6 @@ def tile_attention_pa_kernel(tc, x, qkv_w, qkv_g, qkv_b, out_0, out_1, out_2):
                     w_transposes(k, "w", 1)
                 else:
                     w_transposes(k, "o", 2)
-            if i == 0:
-                gps = psum.tile([P, P], BF16, name="gps", tag="o", bufs=2)
-                nc.tensor.transpose(out=gps[:], in_=gbraw[:], identity=identb[:])
-                nc.scalar.copy(out=gg[:, :, 0], in_=gps[:, 0:NT])
-                nc.scalar.activation(out=gg[:, :, 1], in_=gps[:, 0:NT], func=AF.Copy, scale=-1.0)
-                nc.scalar.copy(out=bb[:], in_=gps[:, 32 : 32 + NT])
             if to_quantize:
                 w_quantize(to_quantize[0])
             if i + FIRST_SORTED < NT:

@@ -364,6 +364,10 @@ def tile_attention_pa_kernel(tc, x, qkv_w, qkv_g, qkv_b, out_0, out_1, out_2):
                 w_quantize(to_quantize[0])
             if i + FIRST_SORTED < NT:
                 sort_words(i + FIRST_SORTED, st[i][:, 1, 0:1])
+            late = NT - 4 <= i < NT - 2
+            if late:
+                back_transposes(j)
+                finish(j, 0, True, 0, 1)
             if i < NT:
                 aggregate(i)
             for k in to_quantize[1:]:
@@ -372,7 +376,7 @@ def tile_attention_pa_kernel(tc, x, qkv_w, qkv_g, qkv_b, out_0, out_1, out_2):
             for k in now_t:
                 evacuate(("w", k), scopy if (k < 6 and k % 2 == 1) else vcopy)
                 to_quantize.append(k)
-            if back:
+            if back and not late:
                 back_transposes(j)
             tail = i >= NT - 2
             halves = j >= NT - 1
@@ -402,7 +406,10 @@ def tile_attention_pa_kernel(tc, x, qkv_w, qkv_g, qkv_b, out_0, out_1, out_2):
                 if i < NT:
                     chain_first(i)
                 if back and not tail:
-                    finish(j, 0, False, 0, 2)
+                    if late:
+                        finish(j, 0, False, 1, 1)
+                    else:
+                        finish(j, 0, False, 0, 2)
                 if i < NT:
                     chain_second(i)
                 if back and not tail:

@@ -20,7 +20,7 @@ ALU = mybir.AluOpType
 P = 128
 NT = HQKV // P
 NPASS = DIM // 512
-AHEAD = 10
+AHEAD = 22
 LAG = 2
 FIRST_SORTED = 6
 FT = list(range(21)) + [22, 21, 23]

@@ -72,10 +72,10 @@ def tile_attention_pa_kernel(tc, x, qkv_w, qkv_g, qkv_b, out_0, out_1, out_2):
         ot = {}
 
         def load_x(b):
+            t = raw.tile([P, 2, DIM], BF16, name="xraw%d" % b, tag="xraw%d" % b)
+            nc.sync.dma_start(out=t[:], in_=x[b, :, :].rearrange("(p e) k -> p e k", e=2))
             for e in range(2):
-                t = raw.tile([P, DIM], BF16, name="xraw%d%d" % (b, e), tag="xraw%d%d" % (b, e))
-                nc.sync.dma_start(out=t[:], in_=x[b, :, :].rearrange("(p e) k -> p e k", e=2)[:, e, :])
-                xraw[(b, e)] = t
+                xraw[(b, e)] = t[:, e, :]
 
         def load_x_by_pass(b):
             for g in range(NPASS):
@@ -90,6 +90,14 @@ def tile_attention_pa_kernel(tc, x, qkv_w, qkv_g, qkv_b, out_0, out_1, out_2):
             t = raw.tile([P, DIM], BF16, name="wraw", tag="wraw", bufs=AHEAD + 2)
             nc.sync.dma_start(out=t[:], in_=qkv_w[FT[i] * P : (FT[i] + 1) * P, :])
             wraw[i] = t
+
+        def load_w_pair(i):
+            t = raw.tile([P, 2, DIM], BF16, name="wraw2", tag="wraw2", bufs=7)
+            nc.sync.dma_start(
+                out=t[:], in_=qkv_w[FT[i] * P : (FT[i] + 2) * P, :].rearrange("(t p) k -> p t k", t=2)
+            )
+            for n in range(2):
+                wraw[i + n] = t[:, n, :]
 
         def transpose_words(dst, words, first):
             nc.tensor.transpose(out=dst, in_=words[:, first : first + 255 : 2], identity=identf[:])
@@ -123,7 +131,7 @@ def tile_attention_pa_kernel(tc, x, qkv_w, qkv_g, qkv_b, out_0, out_1, out_2):
             t0 = psum.tile([P, 512], F32, name="tp_x0", tag="y", bufs=5)
             t1 = psum.tile([P, 512], F32, name="tp_x1", tag="o", bufs=2)
             for e in range(2):
-                words = xraw[(b, e)][:].bitcast(F32)
+                words = xraw[(b, e)].bitcast(F32)
                 for g, t in enumerate((t0, t1)):
                     for u in range(2):
                         s = 2 * e + u
@@ -294,7 +302,10 @@ def tile_attention_pa_kernel(tc, x, qkv_w, qkv_g, qkv_b, out_0, out_1, out_2):
             nc.sync.dma_start(out=gbraw[r0 : r0 + 16, :], in_=rows[0:16, :])
             nc.sync.dma_start(out=gbraw[r0 + 16 : r0 + NT, :], in_=rows[16:NT, :])
         for i in range(2, AHEAD):
-            load_w(i)
+            if not 6 <= i < 20:
+                load_w(i)
+            elif i % 2 == 0:
+                load_w_pair(i)
 
         vcopy = nc.vector.tensor_copy
         scopy = nc.scalar.copy

@@ -297,11 +297,12 @@ def tile_attention_pa_kernel(tc, x, qkv_w, qkv_g, qkv_b, out_0, out_1, out_2):
         load_x(2)
         load_x_by_pass(3)
         load_w(1)
-        for r0, src in ((0, qkv_g), (32, qkv_b)):
-            rows = src.rearrange("(c p) -> c p", p=P)
-            nc.sync.dma_start(out=gbraw[r0 : r0 + 16, :], in_=rows[0:16, :])
-            nc.sync.dma_start(out=gbraw[r0 + 16 : r0 + NT, :], in_=rows[16:NT, :])
         for i in range(2, AHEAD):
+            if i == 4:
+                for r0, src in ((0, qkv_g), (32, qkv_b)):
+                    rows = src.rearrange("(c p) -> c p", p=P)
+                    nc.sync.dma_start(out=gbraw[r0 : r0 + 16, :], in_=rows[0:16, :])
+                    nc.sync.dma_start(out=gbraw[r0 + 16 : r0 + NT, :], in_=rows[16:NT, :])
             if not 6 <= i < 20:
                 load_w(i)
             elif i % 2 == 0:
@@ -335,11 +336,6 @@ def tile_attention_pa_kernel(tc, x, qkv_w, qkv_g, qkv_b, out_0, out_1, out_2):
         w_transposes(1, "w", 1)
         evacuate(("w", 1), scopy)
         x_quantize(3, 1)
-        gps = psum.tile([P, P], BF16, name="gps", tag="o", bufs=2)
-        nc.tensor.transpose(out=gps[:], in_=gbraw[:], identity=identb[:])
-        nc.scalar.copy(out=gg[:, :, 0], in_=gps[:, 0:NT])
-        nc.scalar.activation(out=gg[:, :, 1], in_=gps[:, 0:NT], func=AF.Copy, scale=-1.0)
-        nc.scalar.copy(out=bb[:], in_=gps[:, 32 : 32 + NT])
 
         def fin_on_vector(j):
             return j % 2 == 1 or j >= 18
@@ -371,6 +367,12 @@ def tile_attention_pa_kernel(tc, x, qkv_w, qkv_g, qkv_b, out_0, out_1, out_2):
                     w_transposes(k, "w", 1)
                 else:
                     w_transposes(k, "o", 2)
+            if i == 0:
+                gps = psum.tile([P, P], BF16, name="gps", tag="o", bufs=2)
+                nc.tensor.transpose(out=gps[:], in_=gbraw[:], identity=identb[:])
+                nc.scalar.copy(out=gg[:, :, 0], in_=gps[:, 0:NT])
+                nc.scalar.activation(out=gg[:, :, 1], in_=gps[:, 0:NT], func=AF.Copy, scale=-1.0)
+                nc.scalar.copy(out=bb[:], in_=gps[:, 32 : 32 + NT])
             if to_quantize:
                 w_quantize(to_quantize[0])
             if i + FIRST_SORTED < NT:

from contextlib import ExitStack

import concourse.mybir as mybir
from concourse.masks import make_identity

B, N, DIM, H, KD, D = 4, 256, 1024, 12, 64, 128
HD = 2 * KD + D
HQKV = H * HD
EPS = 1e-5
FLOPS = 2 * B * N * DIM * HQKV

F32 = mybir.dt.float32
BF16 = mybir.dt.bfloat16
U32 = mybir.dt.uint32
U8 = mybir.dt.uint8
E5X4 = mybir.dt.float8_e5m2_x4
AF = mybir.ActivationFunctionType
ALU = mybir.AluOpType

P = 128
NT = HQKV // P
NPASS = DIM // 512
AHEAD = 22
LAG = 2
FIRST_SORTED = 6
FT = list(range(21)) + [22, 21, 23]


def tile_attention_pa_kernel(tc, x, qkv_w, qkv_g, qkv_b, out_0, out_1, out_2):
    nc = tc.nc
    with ExitStack() as ctx:
        const = ctx.enter_context(tc.tile_pool(name="const", bufs=1))
        raw = ctx.enter_context(tc.tile_pool(name="raw", bufs=1))
        work = ctx.enter_context(tc.tile_pool(name="work", bufs=3))
        psum = ctx.enter_context(tc.psum_pool(name="psum", bufs=2))
        ctx.enter_context(tc.manual_schedule())

        one = const.tile([P, 1], F32, name="one", tag="one")
        nc.vector.memset(one[:], 1.0)
        warm = const.tile([P, 1], F32, name="warm", tag="warm")
        nc.scalar.activation(out=warm[:], in_=one[:], func=AF.Abs_reciprocal_sqrt)

        gbraw = const.tile([P, P], BF16, name="gbraw", tag="gbraw")
        nc.vector.memset(gbraw[:], 0.0)

        identf = const.tile([P, P], F32, name="identf", tag="identf")
        make_identity(nc, identf[:])
        identb = const.tile([P, P], BF16, name="identb", tag="identb")
        make_identity(nc, identb[:])

        xc = const.tile([P, NPASS, B * N], U32, name="xc", tag="xc", align_bytes=256)
        xs = const.tile([P, NPASS, B * N], U8, name="xs", tag="xs", align_bytes=256)
        gg = const.tile([P, NT, 2], F32, name="gg", tag="gg")
        bb = const.tile([P, NT], F32, name="bb", tag="bb")

        xraw = {}
        wraw = {}
        wsort = {}
        bank = {}
        grp = {}
        wc = {}
        ws = {}
        yb = {}
        st = {}
        mv = {}
        rstd = {}
        nmg = {}
        sc2 = {}
        bia = {}
        zt = {}
        ob = {}
        ot = {}

        def load_x(b):
            t = raw.tile([P, 2, DIM], BF16, name="xraw%d" % b, tag="xraw%d" % b)
            nc.sync.dma_start(out=t[:], in_=x[b, :, :].rearrange("(p e) k -> p e k", e=2))
            for e in range(2):
                xraw[(b, e)] = t[:, e, :]

        def load_x_by_pass(b):
            for g in range(NPASS):
                for e in range(2):
                    t = raw.tile([P, 512], BF16, name="xraw%d%d%d" % (b, e, g), tag="xraw%d%d%d" % (b, e, g))
                    nc.sync.dma_start(
                        out=t[:], in_=x[b, :, :].rearrange("(p e) k -> p e k", e=2)[:, e, 512 * g : 512 * (g + 1)]
                    )
                    xraw[(b, e, g)] = t

        def load_w(i):
            t = raw.tile([P, DIM], BF16, name="wraw", tag="wraw", bufs=AHEAD + 2)
            nc.sync.dma_start(out=t[:], in_=qkv_w[FT[i] * P : (FT[i] + 1) * P, :])
            wraw[i] = t

        def load_w_pair(i):
            t = raw.tile([P, 2, DIM], BF16, name="wraw2", tag="wraw2", bufs=7)
            nc.sync.dma_start(
                out=t[:], in_=qkv_w[FT[i] * P : (FT[i] + 2) * P, :].rearrange("(t p) k -> p t k", t=2)
            )
            for n in range(2):
                wraw[i + n] = t[:, n, :]

        def transpose_words(dst, words, first):
            nc.tensor.transpose(out=dst, in_=words[:, first : first + 255 : 2], identity=identf[:])

        def sort_words(i, count):
            t = raw.tile([P, DIM], BF16, name="wsort", tag="wsort", bufs=4)
            for g in range(NPASS):
                nc.gpsimd.tensor_scalar(
                    out=t[:, 512 * g : 512 * (g + 1)].rearrange("p (u m e) -> p u m e", u=2, e=2),
                    in0=wraw[i][:, 512 * g : 512 * (g + 1)].rearrange("p (m u e) -> p u m e", u=2, e=2),
                    scalar1=1.0 / 256.0,
                    scalar2=count,
                    op0=ALU.mult,
                    op1=ALU.mult,
                )
            wsort[i] = t

        def x_transposes_by_pass(b):
            t0 = psum.tile([P, 512], F32, name="tp_x0", tag="y", bufs=5)
            t1 = psum.tile([P, 512], F32, name="tp_x1", tag="o", bufs=2)
            for g, t in enumerate((t0, t1)):
                for e in range(2):
                    words = xraw[(b, e, g)][:].bitcast(F32)
                    for u in range(2):
                        s = 2 * e + u
                        transpose_words(t[:, s * P : (s + 1) * P], words, u)
            bank[("x", b, 0)] = t0
            bank[("x", b, 1)] = t1

        def x_transposes(b):
            t0 = psum.tile([P, 512], F32, name="tp_x0", tag="y", bufs=5)
            t1 = psum.tile([P, 512], F32, name="tp_x1", tag="o", bufs=2)
            for e in range(2):
                words = xraw[(b, e)].bitcast(F32)
                for g, t in enumerate((t0, t1)):
                    for u in range(2):
                        s = 2 * e + u
                        transpose_words(t[:, s * P : (s + 1) * P], words, 256 * g + u)
            bank[("x", b, 0)] = t0
            bank[("x", b, 1)] = t1

        def w_transposes(i, tag, bufs):
            t = psum.tile([P, 512], F32, name="tp_" + tag, tag=tag, bufs=bufs)
            if i in wsort:
                words = wsort[i][:].bitcast(F32)
                for s in range(4):
                    nc.tensor.transpose(
                        out=t[:, s * P : (s + 1) * P], in_=words[:, s * P : (s + 1) * P], identity=identf[:]
                    )
            else:
                words = wraw[i][:].bitcast(F32)
                for g in range(2):
                    for u in range(2):
                        s = 2 * g + u
                        transpose_words(t[:, s * P : (s + 1) * P], words, 256 * g + u)
            bank[("w", i)] = t

        def evacuate(key, copy):
            t = work.tile([P, 1024], BF16, name="grp", tag="grp", bufs=4, align_bytes=256)
            copy(
                out=t[:].bitcast(F32).rearrange("p (a r u) -> p a r u", a=2, u=2),
                in_=bank[key][:].rearrange("p (a u r) -> p a r u", a=2, u=2),
            )
            grp[key] = t

        def x_quantize(b, g):
            cols = slice(256 * b, 256 * (b + 1))
            nc.vector.quantize_mx(
                out=xc[:, g, cols].bitcast(E5X4), scales=xs[:, g, cols], in_=grp[("x", b, g)][:]
            )

        def w_quantize(i):
            c = work.tile([P, 256], U32, name="wc", tag="wc", bufs=6, align_bytes=256)
            s = work.tile([P, 256], U8, name="ws", tag="ws", bufs=6, align_bytes=256)
            nc.vector.quantize_mx(out=c[:].bitcast(E5X4), scales=s[:], in_=grp[("w", i)][:])
            wc[i] = c
            ws[i] = s

        def multiply(i, halves=(0, 1)):
            for hf in halves:
                y = psum.tile([P, 512], F32, name="y", tag="y", bufs=5)
                for g in range(NPASS):
                    nc.tensor.matmul_mx(
                        out=y[:],
                        lhsT=wc[i][:, g * P : (g + 1) * P].bitcast(E5X4),
                        lhsT_scale=ws[i][:, g * P : (g + 1) * P],
                        rhs=xc[:, g, hf * 512 : (hf + 1) * 512].bitcast(E5X4),
                        rhs_scale=xs[:, g, hf * 512 : (hf + 1) * 512],
                        start=(g == 0),
                        stop=(g == NPASS - 1),
                    )
                yb[(i, hf)] = y

        def stats(i):
            t = work.tile([P, 2, 6], F32, name="st", tag="st", bufs=3)
            for hf in range(2):
                nc.vector.bn_stats(out=t[:, hf, :], in_=yb[(i, hf)][:])
            st[i] = t

        def aggregate(i):
            t = work.tile([P, 2], F32, name="mv", tag="mv", bufs=3)
            nc.vector.bn_aggr(out=t[:], in_=st[i][:].rearrange("p a s -> p (a s)"))
            mv[i] = t

        def chain_first(i):
            t = work.tile([P, 1], F32, name="nmg", tag="nmg", bufs=3)
            nc.scalar.activation(out=t[:], in_=mv[i][:, 0:1], func=AF.Copy, scale=gg[:, FT[i], 1:2])
            nmg[i] = t
            t = work.tile([P, 1], F32, name="rstd", tag="rstd", bufs=3)
            nc.scalar.activation(out=t[:], in_=mv[i][:, 1:2], func=AF.Abs_reciprocal_sqrt, bias=EPS, scale=1.0)
            rstd[i] = t

        def chain_second(i):
            t = work.tile([P, 1], F32, name="sc", tag="sc", bufs=3)
            nc.scalar.activation(out=t[:], in_=gg[:, FT[i], 0:1], func=AF.Copy, scale=rstd[i][:, 0:1])
            sc2[i] = t
            t = work.tile([P, 1], F32, name="bia", tag="bia", bufs=3)
            nc.scalar.activation(
                out=t[:], in_=nmg[i][:], func=AF.Identity, scale=rstd[i][:, 0:1], bias=bb[:, FT[i] : FT[i] + 1]
            )
            bia[i] = t

        def chain_rstd(i):
            t = work.tile([P, 1], F32, name="rstd", tag="rstd", bufs=3)
            nc.scalar.activation(out=t[:], in_=mv[i][:, 1:2], func=AF.Abs_reciprocal_sqrt, bias=EPS, scale=1.0)
            rstd[i] = t

        def chain_scales(i):
            t = work.tile([P, 2], F32, name="scn", tag="scn", bufs=3)
            nc.scalar.activation(out=t[:], in_=gg[:, FT[i], :], func=AF.Copy, scale=rstd[i][:, 0:1])
            sc2[i] = t

        def chain_bias(i):
            t = work.tile([P, 1], F32, name="bia", tag="bia", bufs=3)
            nc.scalar.activation(
                out=t[:], in_=mv[i][:, 0:1], func=AF.Identity, scale=sc2[i][:, 1:2], bias=bb[:, FT[i] : FT[i] + 1]
            )
            bia[i] = t

        def normalise(i, hf, on_vector):
            z = work.tile([P, 512], F32, name="z%d" % hf, tag="z%d" % hf, bufs=4)
            if on_vector:
                nc.vector.tensor_scalar(
                    out=z[:], in0=yb[(i, hf)][:], scalar1=sc2[i][:, 0:1], scalar2=bia[i][:, 0:1],
                    op0=ALU.mult, op1=ALU.add,
                )
            else:
                nc.scalar.activation(
                    out=z[:], in_=yb[(i, hf)][:], func=AF.Identity, scale=sc2[i][:, 0:1], bias=bia[i][:, 0:1]
                )
            zt[(i, hf)] = z

        def back_transposes(i):
            for hf in range(2):
                third = i >= NT - 6 and (2 * i + hf) % 3 == 2
                t = psum.tile([P, 512], F32, name="ob", tag="w" if third else "o", bufs=1 if third else 2)
                for j in range(4):
                    nc.tensor.transpose(
                        out=t[:, j * P : (j + 1) * P],
                        in_=zt[(i, hf)][:, j * P : (j + 1) * P],
                        identity=identf[:],
                    )
                ob[(i, hf)] = t

        def finish(i, hf, on_vector, j0=0, nj=4):
            copy = nc.vector.tensor_copy if on_vector else nc.scalar.copy
            if i not in ot:
                ot[i] = work.tile([P, 1024], F32, name="ot", tag="ot", bufs=5)
            o = ot[i]
            src = ob[(i, hf)][:, P * j0 : P * (j0 + nj)]
            if FT[i] % 2 == 0:
                copy(
                    out=o[:].rearrange("p (s j d) -> p s j d", s=2, j=8)[:, :, 4 * hf + j0 : 4 * hf + j0 + nj, :],
                    in_=src.rearrange("p (j s d) -> p s j d", j=nj, s=2),
                )
            else:
                copy(out=o[:, 512 * hf + P * j0 : 512 * hf + P * (j0 + nj)], in_=src)

        def store(i, b0, nb):
            h = FT[i] // 2
            o = ot[i]
            if FT[i] % 2 == 0:
                for s, dst in enumerate((out_0, out_1)):
                    nc.sync.dma_start(
                        out=dst[b0 : b0 + nb, h, :, :].rearrange("b (p e) d -> p b (e d)", e=2),
                        in_=o[:, 512 * s + 128 * b0 : 512 * s + 128 * (b0 + nb)].rearrange("p (b f) -> p b f", b=nb),
                    )
            else:
                nc.sync.dma_start(
                    out=out_2[b0 : b0 + nb, h, :, :].rearrange("b (p e) d -> p b (e d)", e=2),
                    in_=o[:, 256 * b0 : 256 * (b0 + nb)].rearrange("p (b f) -> p b f", b=nb),
                )

        load_x(0)
        load_x(1)
        load_w(0)
        load_x(2)
        load_x_by_pass(3)
        load_w(1)
        for i in range(2, AHEAD):
            if i == 4:
                for r0, src in ((0, qkv_g), (32, qkv_b)):
                    rows = src.rearrange("(c p) -> c p", p=P)
                    nc.sync.dma_start(out=gbraw[r0 : r0 + 16, :], in_=rows[0:16, :])
                    nc.sync.dma_start(out=gbraw[r0 + 16 : r0 + NT, :], in_=rows[16:NT, :])
            if not 6 <= i < 20:
                load_w(i)
            elif i % 2 == 0:
                load_w_pair(i)

        vcopy = nc.vector.tensor_copy
        scopy = nc.scalar.copy
        x_transposes(0)
        evacuate(("x", 0, 0), vcopy)
        evacuate(("x", 0, 1), scopy)
        x_transposes(1)
        evacuate(("x", 1, 0), vcopy)
        evacuate(("x", 1, 1), scopy)
        x_quantize(0, 0)
        x_quantize(0, 1)
        w_transposes(0, "w", 1)
        evacuate(("w", 0), scopy)
        x_quantize(1, 0)
        x_quantize(1, 1)
        w_quantize(0)
        x_transposes(2)
        evacuate(("x", 2, 1), scopy)
        evacuate(("x", 2, 0), scopy)
        x_transposes_by_pass(3)
        evacuate(("x", 3, 0), vcopy)
        evacuate(("x", 3, 1), scopy)
        x_quantize(2, 1)
        x_quantize(2, 0)
        x_quantize(3, 0)
        multiply(0, (0,))
        w_transposes(1, "w", 1)
        evacuate(("w", 1), scopy)
        x_quantize(3, 1)

        def fin_on_vector(j):
            return j % 2 == 1 or j >= 18

        def norm_on_vector(i):
            return i >= NT - 2

        next_t = 2
        next_load = AHEAD
        to_quantize = [1]
        for i in range(NT + LAG):
            j = i - LAG
            back = 0 <= j < NT
            now_t = []
            for k in range(2 if i < LAG else 1):
                if next_t < NT:
                    now_t.append(next_t)
                    next_t += 1
                    if next_load < NT:
                        load_w(next_load)
                        next_load += 1
            if i < NT:
                multiply(i, (1,) if i == 0 else (0, 1))
                stats(i)
            if 0 <= i - 1 < NT and norm_on_vector(i - 1):
                normalise(i - 1, 1, True)
            for n, k in enumerate(now_t):
                if n == 0:
                    w_transposes(k, "w", 1)
                else:
                    w_transposes(k, "o", 2)
            if i == 0:
                gps = psum.tile([P, P], BF16, name="gps", tag="o", bufs=2)
                nc.tensor.transpose(out=gps[:], in_=gbraw[:], identity=identb[:])
                nc.scalar.copy(out=gg[:, :, 0], in_=gps[:, 0:NT])
                nc.scalar.activation(out=gg[:, :, 1], in_=gps[:, 0:NT], func=AF.Copy, scale=-1.0)
                nc.scalar.copy(out=bb[:], in_=gps[:, 32 : 32 + NT])
            if to_quantize:
                w_quantize(to_quantize[0])
            if i + FIRST_SORTED < NT:
                sort_words(i + FIRST_SORTED, st[i][:, 1, 0:1])
            late = NT - 4 <= i < NT - 2
            if late:
                back_transposes(j)
                finish(j, 0, True, 0, 1)
            if i < NT:
                aggregate(i)
            for k in to_quantize[1:]:
                w_quantize(k)
            to_quantize = []
            for k in now_t:
                evacuate(("w", k), scopy if (k < 6 and k % 2 == 1) else vcopy)
                to_quantize.append(k)
            if back and not late:
                back_transposes(j)
            tail = i >= NT - 2
            halves = j >= NT - 1
            on_v = back and fin_on_vector(j)
            if tail and back:
                finish(j, 0, False)
                if halves:
                    store(j, 0, 2)
                if j == NT - 1:
                    finish(j, 1, on_v, 0, 2)
                    store(j, 2, 1)
                    finish(j, 1, on_v, 2, 2)
                else:
                    finish(j, 1, on_v)
            level = back and j < 18
            if level:
                chain_rstd(i)
                finish(j, 0, False, 0, 2)
                chain_scales(i)
                finish(j, 0, False, 2, 2)
                chain_bias(i)
                nv = 3 if j % 2 == 1 else 0
                if nv:
                    finish(j, 1, True, 0, nv)
                finish(j, 1, False, nv, 4 - nv)
            else:
                if i < NT:
                    chain_first(i)
                if back and not tail:
                    if late:
                        finish(j, 0, False, 1, 1)
                    else:
                        finish(j, 0, False, 0, 2)
                if i < NT:
                    chain_second(i)
                if back and not tail:
                    finish(j, 0, False, 2, 2)
                    finish(j, 1, on_v)
            if back:
                if j == NT - 1:
                    store(j, 3, 1)
                elif halves:
                    store(j, 2, 2)
                else:
                    store(j, 0, B)
            if i < NT:
                normalise(i, 0, False)
                if not norm_on_vector(i):
                    normalise(i, 1, False)
